import numpy as np
import ml_dtypes


def mxq(x, axis, fmt="e4m3"):
    dtype, down = {"e4m3": (ml_dtypes.float8_e4m3fn, 7), "e5m2": (ml_dtypes.float8_e5m2, 14)}[fmt]
    v = np.moveaxis(np.asarray(x, np.float32).astype(ml_dtypes.bfloat16).astype(np.float64), axis, -1)
    blocks = v.reshape(v.shape[:-1] + (-1, 32))
    amax = np.abs(blocks).max(-1, keepdims=True)
    byte = np.maximum(np.where(amax > 0, np.frexp(amax)[1] - 1 + 127, 0) - down, 1)
    scale = np.exp2(byte - 127.0)
    codes = (blocks / scale).astype(np.float32).astype(dtype).astype(np.float64)
    return np.moveaxis((codes * scale).reshape(v.shape), -1, axis)


WIDE = False


def mx_kscale(k):
    if not WIDE:
        return np.ones(k)
    levels = np.array([20, -20, 10, -10, 0])
    a = np.random.permutation(np.resize(levels, k // 512 * 4)).reshape(k // 512, 4)
    idx = np.arange(k)
    return np.exp2(a[idx // 512, idx % 128 // 32])


BF16 = ml_dtypes.bfloat16


def bf(x):
    return np.asarray(x, np.float32).astype(BF16)


def f64(x):
    return np.asarray(x).astype(np.float64)


B, C, H, W, R = 2, 256, 128, 64, 4
N = H * W
NOISE = 0.5
GSCALE = 64.0


def mix(a, z):
    return sum(a[:, :, r, None] * z[:, r, None, :] for r in range(R))


def softmax(s):
    e = np.exp(s - s.max(-1, keepdims=True))
    return e / e.sum(-1, keepdims=True)


def setup_inputs():
    s = mx_kscale(N)
    z = np.random.standard_normal((B, R, N))
    a1 = np.random.standard_normal((B, C, R)) / np.sqrt(R)
    a2 = np.random.standard_normal((B, C, R)) / np.sqrt(R)
    x1 = mix(a1, z) + NOISE * np.random.standard_normal((B, C, N))
    x2 = mix(a2, z) + NOISE * np.random.standard_normal((B, C, N))
    u1 = a1 / np.sqrt((a1 * a1).sum(2, keepdims=True) + NOISE * NOISE)
    u2 = a2 / np.sqrt((a2 * a2).sum(2, keepdims=True) + NOISE * NOISE)
    logits1 = mix(u1 + u2, u1.transpose(0, 2, 1))
    logits2 = mix(u2 + u1, u2.transpose(0, 2, 1))
    x1 = x1 * s[None, None, :]
    g = np.random.standard_normal((B, N, C)) * np.exp2(np.random.randint(-12, 1, (B, N, 1))) * GSCALE / s[None, :, None]
    return {"logits1": bf(logits1), "logits2": bf(logits2),
            "x1": bf(x1.reshape(B, C, H, W)), "x2": bf(x2.reshape(B, C, H, W)),
            "grad_out": bf(g.reshape(B, C, H, W))}


def reference(logits1, logits2, x1, x2, grad_out):
    g = f64(grad_out).reshape(B, N, C)
    x = f64(x1).reshape(B, C, N)
    p = softmax(f64(logits1))
    gq = mxq(g, 1, "e5m2")
    xq = mxq(x, 2, "e4m3")
    d = gq.transpose(0, 2, 1) @ xq.transpose(0, 2, 1)
    return p * (d - (p * d).sum(-1, keepdims=True))

@@ -1,0 +1,246 @@
+from contextlib import ExitStack
+
+import concourse.mybir as mybir
+from concourse.masks import make_identity
+
+F32 = mybir.dt.float32
+BF16 = mybir.dt.bfloat16
+I32 = mybir.dt.int32
+U32 = mybir.dt.uint32
+U8 = mybir.dt.uint8
+E4M3_X4 = mybir.dt.float8_e4m3fn_x4
+E5M2_X4 = mybir.dt.float8_e5m2_x4
+ALU = mybir.AluOpType
+ACT = mybir.ActivationFunctionType
+AXIS = mybir.AxisListType
+
+B = 2
+C = 256
+N = 8192
+
+P = 128
+PACK = 4
+K_PASS = P * PACK
+C_TILES = C // P
+PASS_WORDS = K_PASS // 2
+MOVING = 512
+
+ROUND = 2
+ROUNDS_PER_BATCH = N // (K_PASS * ROUND)
+ROUNDS = B * ROUNDS_PER_BATCH
+PASSES_PER_BATCH = N // K_PASS
+X_LOAD_ROUNDS = 2
+X_LOAD_N = X_LOAD_ROUNDS * ROUND * K_PASS
+X_LOADS = ROUNDS // X_LOAD_ROUNDS
+
+G_COLS_VECTOR = 160
+
+FLOPS = 2 * B * C * C * N
+BYTES = 2 * B * C * C + 2 * 2 * B * C * N + 4 * B * C * C
+
+
+def tile_interfusion_pb_k_kernel(tc, logits1, logits2, x1, x2, grad_out, out):
+    nc = tc.nc
+    with ExitStack() as ctx:
+        ctx.enter_context(tc.manual_schedule())
+        resident = ctx.enter_context(tc.tile_pool(name="resident", bufs=1))
+        stage = ctx.enter_context(tc.tile_pool(name="stage", bufs=3))
+        results = ctx.enter_context(tc.tile_pool(name="results", bufs=2))
+        xt_banks = ctx.enter_context(tc.psum_pool(name="xt_banks", bufs=2 * ROUND))
+        d_banks = ctx.enter_context(tc.psum_pool(name="d_banks", bufs=B))
+
+        logits = resident.tile([P, B * C_TILES, C], BF16)
+        nc.sync.dma_start(out=logits[:], in_=logits1.rearrange("b (ct p) j -> p (b ct) j", p=P))
+
+        x_view = x1.rearrange("b (ct p) h w -> b p ct (h w)", p=P)
+        x_raw = {}
+
+        def load_x(load):
+            b, part = divmod(load, X_LOADS // B)
+            tile = resident.tile([P, C_TILES * X_LOAD_N], BF16, name="x_raw%d" % load)
+            nc.sync.dma_start(
+                out=tile[:].rearrange("p (ct n) -> p ct n", ct=C_TILES),
+                in_=x_view[b, :, :, part * X_LOAD_N : (part + 1) * X_LOAD_N],
+            )
+            x_raw[load] = tile
+
+        g_view = grad_out.rearrange("b a h w -> b (a h w)").rearrange(
+            "b (r g u q e c) -> b r q (g u) (e c)", g=ROUND, u=2, q=P, e=2, c=C
+        )
+        g_raw = {}
+
+        def load_g(r):
+            b, rb = divmod(r, ROUNDS_PER_BATCH)
+            tile = resident.tile([P, ROUND, PACK, C], BF16, name="g_raw%d" % r)
+            nc.sync.dma_start(
+                out=tile[:].rearrange("p g (u e) c -> p (g u) (e c)", e=2), in_=g_view[b, rb]
+            )
+            g_raw[r] = tile
+
+        load_x(0)
+        for load in range(X_LOADS):
+            if load + 1 < X_LOADS:
+                load_x(load + 1)
+            for r in range(load * X_LOAD_ROUNDS, (load + 1) * X_LOAD_ROUNDS):
+                load_g(r)
+
+        identity = resident.tile([P, P], F32)
+        make_identity(nc, identity[:])
+
+        x_codes = {}
+        x_scales = {}
+        for b in range(B):
+            codes = resident.tile([P, (PASSES_PER_BATCH + 1) * C], U32, name="x_codes%d" % b, align_bytes=64)
+            scales = resident.tile([P, (PASSES_PER_BATCH + 1) * C], U8, name="x_scales%d" % b, align_bytes=64)
+            nc.vector.memset(codes[:].bitcast(I32)[:, 0:C], 0)
+            nc.vector.memset(scales[:].bitcast(I32)[:, 0 : C // 4], 0)
+            x_codes[b] = codes
+            x_scales[b] = scales
+
+        row_max = resident.tile([P, B * C_TILES], F32)
+        neg_max = resident.tile([P, B * C_TILES], F32)
+        row_sum = resident.tile([P, B * C_TILES], F32)
+        inv_sum = resident.tile([P, B * C_TILES], F32)
+        prob = resident.tile([P, B * C_TILES, C], F32)
+        nc.vector.tensor_reduce(out=row_max[:], in_=logits[:], axis=AXIS.X, op=ALU.max)
+        nc.vector.tensor_scalar_mul(out=neg_max[:], in0=row_max[:], scalar1=-1.0)
+        for i in range(B * C_TILES):
+            nc.scalar.activation(
+                out=prob[:, i, :],
+                in_=logits[:, i, :],
+                func=ACT.Exp,
+                bias=neg_max[:, i : i + 1],
+                scale=1.0,
+                accum_out=row_sum[:, i : i + 1],
+            )
+        nc.vector.reciprocal(out=inv_sum[:], in_=row_sum[:])
+        for i in range(B * C_TILES):
+            nc.vector.tensor_scalar_mul(out=prob[:, i, :], in0=prob[:, i, :], scalar1=inv_sum[:, i : i + 1])
+
+        xt = {}
+        x_grouped = {}
+        g_grouped = {}
+        g_codes = {}
+        g_scales = {}
+        d_acc = {}
+
+        def transpose_x(r):
+            words = x_raw[r // X_LOAD_ROUNDS][:].bitcast(F32)
+            for g in range(ROUND):
+                bank = xt_banks.tile([P, 2, C], F32)
+                first = ((r % X_LOAD_ROUNDS) * ROUND + g) * PASS_WORDS
+                for u in range(2):
+                    for ct in range(C_TILES):
+                        column = ct * (X_LOAD_N // 2) + first + u * P
+                        nc.tensor.transpose(
+                            bank[:, u, ct * P : (ct + 1) * P], words[:, column : column + P], identity[:]
+                        )
+                xt[(r, g)] = bank
+
+        def copy_x(r):
+            grouped = stage.tile([P, ROUND * C * PACK], BF16, name="x_grouped", align_bytes=64)
+            grouped_words = grouped[:].bitcast(F32).rearrange("p (g k u) -> p g k u", g=ROUND, u=2)
+            for g in range(ROUND):
+                nc.scalar.copy(out=grouped_words[:, g], in_=xt[(r, g)][:].rearrange("p u k -> p k u"))
+            x_grouped[r] = grouped
+
+        def regroup_g(r, engine_copy, columns):
+            for g in range(ROUND):
+                engine_copy(
+                    out=g_grouped[r][:, g, columns, :].rearrange("p (c i) t -> p c t i", i=4),
+                    in_=g_raw[r][:, g, :, columns].rearrange("p t (c i) -> p c t i", i=4),
+                )
+
+        def regroup_g_scalar(r):
+            grouped = stage.tile([P, ROUND, C, PACK], BF16, name="g_grouped", align_bytes=64)
+            g_grouped[r] = grouped
+            regroup_g(r, nc.scalar.copy, slice(G_COLS_VECTOR, C))
+
+        def regroup_g_vector(r):
+            regroup_g(r, nc.vector.tensor_copy, slice(0, G_COLS_VECTOR))
+
+        def quantise_x(r):
+            b, rb = divmod(r, ROUNDS_PER_BATCH)
+            slots = slice((1 + rb * ROUND) * C, (1 + (rb + 1) * ROUND) * C)
+            nc.vector.quantize_mx(
+                out=x_codes[b][:, slots].bitcast(E4M3_X4), scales=x_scales[b][:, slots], in_=x_grouped[r][:]
+            )
+
+        def quantise_g(r):
+            codes = stage.tile([P, ROUND * C], U32, name="g_codes", align_bytes=64)
+            scales = stage.tile([P, ROUND * C], U8, name="g_scales", align_bytes=64)
+            nc.vector.quantize_mx(
+                out=codes[:].bitcast(E5M2_X4),
+                scales=scales[:],
+                in_=g_grouped[r][:].rearrange("p g c t -> p (g c t)"),
+            )
+            g_codes[r] = codes
+            g_scales[r] = scales
+
+        def multiply(r):
+            b, rb = divmod(r, ROUNDS_PER_BATCH)
+            for ct in range(C_TILES):
+                if rb == 0:
+                    acc = d_banks.tile([P, MOVING], F32, name="d_acc%d" % ct)
+                    d_acc[(b, ct)] = acc
+                for g in range(ROUND):
+                    k_pass = rb * ROUND + g
+                    rows = slice(g * C + ct * P, g * C + (ct + 1) * P)
+                    window = slice(k_pass * C, k_pass * C + MOVING)
+                    nc.tensor.matmul_mx(
+                        out=d_acc[(b, ct)][:],
+                        lhsT=g_codes[r][:, rows].bitcast(E5M2_X4),
+                        lhsT_scale=g_scales[r][:, rows],
+                        rhs=x_codes[b][:, window].bitcast(E4M3_X4),
+                        rhs_scale=x_scales[b][:, window],
+                        start=(k_pass == 0),
+                        stop=(k_pass == PASSES_PER_BATCH - 1),
+                    )
+
+        dot = resident.tile([P, B * C_TILES], F32)
+
+        def finish(b):
+            for ct in range(C_TILES):
+                i = b * C_TILES + ct
+                weighted = results.tile([P, C], F32, name="weighted")
+                nc.vector.scalar_tensor_tensor(
+                    out=weighted[:],
+                    in0=d_acc[(b, ct)][:, C:MOVING],
+                    scalar=1.0,
+                    in1=prob[:, i, :],
+                    op0=ALU.mult,
+                    op1=ALU.mult,
+                    accum_out=dot[:, i : i + 1],
+                )
+            for ct in range(C_TILES):
+                i = b * C_TILES + ct
+                result = results.tile([P, C], F32, name="result")
+                nc.vector.scalar_tensor_tensor(
+                    out=result[:],
+                    in0=d_acc[(b, ct)][:, C:MOVING],
+                    scalar=dot[:, i : i + 1],
+                    in1=prob[:, i, :],
+                    op0=ALU.subtract,
+                    op1=ALU.mult,
+                )
+                nc.sync.dma_start(out=out[b, ct * P : (ct + 1) * P, :], in_=result[:])
+
+        def live(r):
+            return 0 <= r < ROUNDS
+
+        for i in range(-2, ROUNDS + 2):
+            if live(i - 2):
+                multiply(i - 2)
+            if live(i + 2):
+                transpose_x(i + 2)
+            if live(i + 1):
+                copy_x(i + 1)
+            if live(i):
+                regroup_g_scalar(i)
+                quantise_x(i)
+            if live(i - 1):
+                quantise_g(i - 1)
+            if live(i):
+                regroup_g_vector(i)
+            if live(i - 2) and (i - 2) % ROUNDS_PER_BATCH == ROUNDS_PER_BATCH - 1:
+                finish((i - 2) // ROUNDS_PER_BATCH)

@@ -22,7 +22,6 @@ P = 128
 PACK = 4
 K_PASS = P * PACK
 C_TILES = C // P
-PASS_WORDS = K_PASS // 2
 MOVING = 512
 
 ROUND = 2
@@ -65,7 +64,7 @@ def tile_interfusion_pb_k_kernel(tc, logits1, logits2, x1, x2, grad_out, out):
             x_raw[load] = tile
 
         g_view = grad_out.rearrange("b a h w -> b (a h w)").rearrange(
-            "b (r g u q e c) -> b r q (g u) (e c)", g=ROUND, u=2, q=P, e=2, c=C
+            "b (r g q t c) -> b r q g (t c)", g=ROUND, q=P, t=PACK, c=C
         )
         g_raw = {}
 
@@ -73,7 +72,7 @@ def tile_interfusion_pb_k_kernel(tc, logits1, logits2, x1, x2, grad_out, out):
             b, rb = divmod(r, ROUNDS_PER_BATCH)
             tile = resident.tile([P, ROUND, PACK, C], BF16, name="g_raw%d" % r)
             nc.sync.dma_start(
-                out=tile[:].rearrange("p g (u e) c -> p (g u) (e c)", e=2), in_=g_view[b, rb]
+                out=tile[:].rearrange("p g t c -> p g (t c)"), in_=g_view[b, rb]
             )
             g_raw[r] = tile
 
@@ -125,15 +124,15 @@ def tile_interfusion_pb_k_kernel(tc, logits1, logits2, x1, x2, grad_out, out):
         d_acc = {}
 
         def transpose_x(r):
-            words = x_raw[r // X_LOAD_ROUNDS][:].bitcast(F32)
+            words = x_raw[r // X_LOAD_ROUNDS][:].bitcast(F32).rearrange("p (q u) -> p q u", u=2)
             for g in range(ROUND):
                 bank = xt_banks.tile([P, 2, C], F32)
-                first = ((r % X_LOAD_ROUNDS) * ROUND + g) * PASS_WORDS
+                first = ((r % X_LOAD_ROUNDS) * ROUND + g) * P
                 for u in range(2):
                     for ct in range(C_TILES):
-                        column = ct * (X_LOAD_N // 2) + first + u * P
+                        column = ct * (X_LOAD_N // PACK) + first
                         nc.tensor.transpose(
-                            bank[:, u, ct * P : (ct + 1) * P], words[:, column : column + P], identity[:]
+                            bank[:, u, ct * P : (ct + 1) * P], words[:, column : column + P, u], identity[:]
                         )
                 xt[(r, g)] = bank
 

@@ -41,7 +41,6 @@ BYTES = 2 * B * C * C + 2 * 2 * B * C * N + 4 * B * C * C
 def tile_interfusion_pb_k_kernel(tc, logits1, logits2, x1, x2, grad_out, out):
     nc = tc.nc
     with ExitStack() as ctx:
-        ctx.enter_context(tc.manual_schedule())
         resident = ctx.enter_context(tc.tile_pool(name="resident", bufs=1))
         stage = ctx.enter_context(tc.tile_pool(name="stage", bufs=3))
         results = ctx.enter_context(tc.tile_pool(name="results", bufs=2))

@@ -20,19 +20,25 @@ N = 8192
 
 P = 128
 PACK = 4
+PAIRS = PACK // 2
 K_PASS = P * PACK
+PASSES = N // K_PASS
 C_TILES = C // P
-MOVING = 512
+ROW_TILES = B * C_TILES
+MOVING = 2 * C
 
 ROUND = 2
-ROUNDS_PER_BATCH = N // (K_PASS * ROUND)
+ROUNDS_PER_BATCH = PASSES // ROUND
 ROUNDS = B * ROUNDS_PER_BATCH
-PASSES_PER_BATCH = N // K_PASS
 X_LOAD_ROUNDS = 2
 X_LOAD_N = X_LOAD_ROUNDS * ROUND * K_PASS
 X_LOADS = ROUNDS // X_LOAD_ROUNDS
 
+X_AHEAD = 2
+MX_BEHIND = 2
+
 G_COLS_VECTOR = 160
+RUN = 4
 
 FLOPS = 2 * B * C * C * N
 BYTES = 2 * B * C * C + 2 * 2 * B * C * N + 4 * B * C * C
@@ -41,13 +47,14 @@ BYTES = 2 * B * C * C + 2 * 2 * B * C * N + 4 * B * C * C
 def tile_interfusion_pb_k_kernel(tc, logits1, logits2, x1, x2, grad_out, out):
     nc = tc.nc
     with ExitStack() as ctx:
+        ctx.enter_context(tc.manual_schedule())
         resident = ctx.enter_context(tc.tile_pool(name="resident", bufs=1))
         stage = ctx.enter_context(tc.tile_pool(name="stage", bufs=3))
         results = ctx.enter_context(tc.tile_pool(name="results", bufs=2))
         xt_banks = ctx.enter_context(tc.psum_pool(name="xt_banks", bufs=2 * ROUND))
         d_banks = ctx.enter_context(tc.psum_pool(name="d_banks", bufs=B))
 
-        logits = resident.tile([P, B * C_TILES, C], BF16)
+        logits = resident.tile([P, ROW_TILES, C], BF16)
         nc.sync.dma_start(out=logits[:], in_=logits1.rearrange("b (ct p) j -> p (b ct) j", p=P))
 
         x_view = x1.rearrange("b (ct p) h w -> b p ct (h w)", p=P)
@@ -63,16 +70,15 @@ def tile_interfusion_pb_k_kernel(tc, logits1, logits2, x1, x2, grad_out, out):
             x_raw[load] = tile
 
         g_view = grad_out.rearrange("b a h w -> b (a h w)").rearrange(
-            "b (r g q t c) -> b r q g (t c)", g=ROUND, q=P, t=PACK, c=C
+            "b (r j q t c) -> b r j q (t c)", j=ROUND, q=P, t=PACK, c=C
         )
         g_raw = {}
 
         def load_g(r):
-            b, rb = divmod(r, ROUNDS_PER_BATCH)
+            b, r_in_batch = divmod(r, ROUNDS_PER_BATCH)
             tile = resident.tile([P, ROUND, PACK, C], BF16, name="g_raw%d" % r)
-            nc.sync.dma_start(
-                out=tile[:].rearrange("p g t c -> p g (t c)"), in_=g_view[b, rb]
-            )
+            for j in range(ROUND):
+                nc.sync.dma_start(out=tile[:, j].rearrange("p t c -> p (t c)"), in_=g_view[b, r_in_batch, j])
             g_raw[r] = tile
 
         load_x(0)
@@ -88,32 +94,32 @@ def tile_interfusion_pb_k_kernel(tc, logits1, logits2, x1, x2, grad_out, out):
         x_codes = {}
         x_scales = {}
         for b in range(B):
-            codes = resident.tile([P, (PASSES_PER_BATCH + 1) * C], U32, name="x_codes%d" % b, align_bytes=64)
-            scales = resident.tile([P, (PASSES_PER_BATCH + 1) * C], U8, name="x_scales%d" % b, align_bytes=64)
+            codes = resident.tile([P, (PASSES + 1) * C], U32, name="x_codes%d" % b, align_bytes=64)
+            scales = resident.tile([P, (PASSES + 1) * C], U8, name="x_scales%d" % b, align_bytes=64)
             nc.vector.memset(codes[:].bitcast(I32)[:, 0:C], 0)
             nc.vector.memset(scales[:].bitcast(I32)[:, 0 : C // 4], 0)
             x_codes[b] = codes
             x_scales[b] = scales
 
-        row_max = resident.tile([P, B * C_TILES], F32)
-        neg_max = resident.tile([P, B * C_TILES], F32)
-        row_sum = resident.tile([P, B * C_TILES], F32)
-        inv_sum = resident.tile([P, B * C_TILES], F32)
-        prob = resident.tile([P, B * C_TILES, C], F32)
+        row_max = resident.tile([P, ROW_TILES], F32)
+        neg_max = resident.tile([P, ROW_TILES], F32)
+        row_sum = resident.tile([P, ROW_TILES], F32)
+        inv_sum = resident.tile([P, ROW_TILES], F32)
+        prob = resident.tile([P, ROW_TILES, C], F32)
         nc.vector.tensor_reduce(out=row_max[:], in_=logits[:], axis=AXIS.X, op=ALU.max)
         nc.vector.tensor_scalar_mul(out=neg_max[:], in0=row_max[:], scalar1=-1.0)
-        for i in range(B * C_TILES):
+        for m in range(ROW_TILES):
             nc.scalar.activation(
-                out=prob[:, i, :],
-                in_=logits[:, i, :],
+                out=prob[:, m, :],
+                in_=logits[:, m, :],
                 func=ACT.Exp,
-                bias=neg_max[:, i : i + 1],
+                bias=neg_max[:, m : m + 1],
                 scale=1.0,
-                accum_out=row_sum[:, i : i + 1],
+                accum_out=row_sum[:, m : m + 1],
             )
         nc.vector.reciprocal(out=inv_sum[:], in_=row_sum[:])
-        for i in range(B * C_TILES):
-            nc.vector.tensor_scalar_mul(out=prob[:, i, :], in0=prob[:, i, :], scalar1=inv_sum[:, i : i + 1])
+        for m in range(ROW_TILES):
+            nc.vector.tensor_scalar_mul(out=prob[:, m, :], in0=prob[:, m, :], scalar1=inv_sum[:, m : m + 1])
 
         xt = {}
         x_grouped = {}
@@ -123,30 +129,30 @@ def tile_interfusion_pb_k_kernel(tc, logits1, logits2, x1, x2, grad_out, out):
         d_acc = {}
 
         def transpose_x(r):
-            words = x_raw[r // X_LOAD_ROUNDS][:].bitcast(F32).rearrange("p (q u) -> p q u", u=2)
-            for g in range(ROUND):
-                bank = xt_banks.tile([P, 2, C], F32)
-                first = ((r % X_LOAD_ROUNDS) * ROUND + g) * P
-                for u in range(2):
+            words = x_raw[r // X_LOAD_ROUNDS][:].bitcast(F32).rearrange("p (q u) -> p q u", u=PAIRS)
+            for j in range(ROUND):
+                bank = xt_banks.tile([P, PAIRS, C], F32)
+                pass_in_load = (r % X_LOAD_ROUNDS) * ROUND + j
+                for u in range(PAIRS):
                     for ct in range(C_TILES):
-                        column = ct * (X_LOAD_N // PACK) + first
+                        first_q = ct * (X_LOAD_N // PACK) + pass_in_load * P
                         nc.tensor.transpose(
-                            bank[:, u, ct * P : (ct + 1) * P], words[:, column : column + P, u], identity[:]
+                            bank[:, u, ct * P : (ct + 1) * P], words[:, first_q : first_q + P, u], identity[:]
                         )
-                xt[(r, g)] = bank
+                xt[(r, j)] = bank
 
         def copy_x(r):
             grouped = stage.tile([P, ROUND * C * PACK], BF16, name="x_grouped", align_bytes=64)
-            grouped_words = grouped[:].bitcast(F32).rearrange("p (g k u) -> p g k u", g=ROUND, u=2)
-            for g in range(ROUND):
-                nc.scalar.copy(out=grouped_words[:, g], in_=xt[(r, g)][:].rearrange("p u k -> p k u"))
+            grouped_words = grouped[:].bitcast(F32).rearrange("p (j k u) -> p j k u", j=ROUND, u=PAIRS)
+            for j in range(ROUND):
+                nc.scalar.copy(out=grouped_words[:, j], in_=xt[(r, j)][:].rearrange("p u k -> p k u"))
             x_grouped[r] = grouped
 
         def regroup_g(r, engine_copy, columns):
-            for g in range(ROUND):
+            for j in range(ROUND):
                 engine_copy(
-                    out=g_grouped[r][:, g, columns, :].rearrange("p (c i) t -> p c t i", i=4),
-                    in_=g_raw[r][:, g, :, columns].rearrange("p t (c i) -> p c t i", i=4),
+                    out=g_grouped[r][:, j, columns, :].rearrange("p (c i) t -> p c t i", i=RUN),
+                    in_=g_raw[r][:, j, :, columns].rearrange("p t (c i) -> p c t i", i=RUN),
                 )
 
         def regroup_g_scalar(r):
@@ -158,8 +164,8 @@ def tile_interfusion_pb_k_kernel(tc, logits1, logits2, x1, x2, grad_out, out):
             regroup_g(r, nc.vector.tensor_copy, slice(0, G_COLS_VECTOR))
 
         def quantise_x(r):
-            b, rb = divmod(r, ROUNDS_PER_BATCH)
-            slots = slice((1 + rb * ROUND) * C, (1 + (rb + 1) * ROUND) * C)
+            b, r_in_batch = divmod(r, ROUNDS_PER_BATCH)
+            slots = slice((1 + r_in_batch * ROUND) * C, (1 + (r_in_batch + 1) * ROUND) * C)
             nc.vector.quantize_mx(
                 out=x_codes[b][:, slots].bitcast(E4M3_X4), scales=x_scales[b][:, slots], in_=x_grouped[r][:]
             )
@@ -167,24 +173,26 @@ def tile_interfusion_pb_k_kernel(tc, logits1, logits2, x1, x2, grad_out, out):
         def quantise_g(r):
             codes = stage.tile([P, ROUND * C], U32, name="g_codes", align_bytes=64)
             scales = stage.tile([P, ROUND * C], U8, name="g_scales", align_bytes=64)
-            nc.vector.quantize_mx(
-                out=codes[:].bitcast(E5M2_X4),
-                scales=scales[:],
-                in_=g_grouped[r][:].rearrange("p g c t -> p (g c t)"),
-            )
+            for j in range(ROUND):
+                nc.vector.quantize_mx(
+                    out=codes[:, j * C : (j + 1) * C].bitcast(E5M2_X4),
+                    scales=scales[:, j * C : (j + 1) * C],
+                    in_=g_grouped[r][:, j].rearrange("p c t -> p (c t)"),
+                )
             g_codes[r] = codes
             g_scales[r] = scales
 
         def multiply(r):
-            b, rb = divmod(r, ROUNDS_PER_BATCH)
-            for ct in range(C_TILES):
-                if rb == 0:
+            b, r_in_batch = divmod(r, ROUNDS_PER_BATCH)
+            if r_in_batch == 0:
+                for ct in range(C_TILES):
                     acc = d_banks.tile([P, MOVING], F32, name="d_acc%d" % ct)
                     d_acc[(b, ct)] = acc
-                for g in range(ROUND):
-                    k_pass = rb * ROUND + g
-                    rows = slice(g * C + ct * P, g * C + (ct + 1) * P)
-                    window = slice(k_pass * C, k_pass * C + MOVING)
+            for j in range(ROUND):
+                k_pass = r_in_batch * ROUND + j
+                window = slice(k_pass * C, k_pass * C + MOVING)
+                for ct in range(C_TILES):
+                    rows = slice(j * C + ct * P, j * C + (ct + 1) * P)
                     nc.tensor.matmul_mx(
                         out=d_acc[(b, ct)][:],
                         lhsT=g_codes[r][:, rows].bitcast(E5M2_X4),
@@ -192,32 +200,32 @@ def tile_interfusion_pb_k_kernel(tc, logits1, logits2, x1, x2, grad_out, out):
                         rhs=x_codes[b][:, window].bitcast(E4M3_X4),
                         rhs_scale=x_scales[b][:, window],
                         start=(k_pass == 0),
-                        stop=(k_pass == PASSES_PER_BATCH - 1),
+                        stop=(k_pass == PASSES - 1),
                     )
 
-        dot = resident.tile([P, B * C_TILES], F32)
+        dot = resident.tile([P, ROW_TILES], F32)
 
         def finish(b):
             for ct in range(C_TILES):
-                i = b * C_TILES + ct
+                m = b * C_TILES + ct
                 weighted = results.tile([P, C], F32, name="weighted")
                 nc.vector.scalar_tensor_tensor(
                     out=weighted[:],
                     in0=d_acc[(b, ct)][:, C:MOVING],
                     scalar=1.0,
-                    in1=prob[:, i, :],
+                    in1=prob[:, m, :],
                     op0=ALU.mult,
                     op1=ALU.mult,
-                    accum_out=dot[:, i : i + 1],
+                    accum_out=dot[:, m : m + 1],
                 )
             for ct in range(C_TILES):
-                i = b * C_TILES + ct
+                m = b * C_TILES + ct
                 result = results.tile([P, C], F32, name="result")
                 nc.vector.scalar_tensor_tensor(
                     out=result[:],
                     in0=d_acc[(b, ct)][:, C:MOVING],
-                    scalar=dot[:, i : i + 1],
-                    in1=prob[:, i, :],
+                    scalar=dot[:, m : m + 1],
+                    in1=prob[:, m, :],
                     op0=ALU.subtract,
                     op1=ALU.mult,
                 )
@@ -226,19 +234,19 @@ def tile_interfusion_pb_k_kernel(tc, logits1, logits2, x1, x2, grad_out, out):
         def live(r):
             return 0 <= r < ROUNDS
 
-        for i in range(-2, ROUNDS + 2):
-            if live(i - 2):
-                multiply(i - 2)
-            if live(i + 2):
-                transpose_x(i + 2)
-            if live(i + 1):
-                copy_x(i + 1)
-            if live(i):
-                regroup_g_scalar(i)
-                quantise_x(i)
-            if live(i - 1):
-                quantise_g(i - 1)
-            if live(i):
-                regroup_g_vector(i)
-            if live(i - 2) and (i - 2) % ROUNDS_PER_BATCH == ROUNDS_PER_BATCH - 1:
-                finish((i - 2) // ROUNDS_PER_BATCH)
+        for s in range(-X_AHEAD, ROUNDS + MX_BEHIND):
+            if live(s - MX_BEHIND):
+                multiply(s - MX_BEHIND)
+            if live(s + X_AHEAD):
+                transpose_x(s + X_AHEAD)
+            if live(s + X_AHEAD - 1):
+                copy_x(s + X_AHEAD - 1)
+            if live(s):
+                regroup_g_scalar(s)
+                quantise_x(s)
+            if live(s - 1):
+                quantise_g(s - 1)
+            if live(s):
+                regroup_g_vector(s)
+            if live(s - MX_BEHIND) and (s - MX_BEHIND) % ROUNDS_PER_BATCH == ROUNDS_PER_BATCH - 1:
+                finish((s - MX_BEHIND) // ROUNDS_PER_BATCH)

@@ -37,7 +37,7 @@ X_LOADS = ROUNDS // X_LOAD_ROUNDS
 X_AHEAD = 2
 MX_BEHIND = 2
 
-G_COLS_VECTOR = 160
+G_COLS_VECTOR = 144
 RUN = 4
 
 FLOPS = 2 * B * C * C * N

from contextlib import ExitStack

import concourse.mybir as mybir
from concourse.masks import make_identity

F32 = mybir.dt.float32
BF16 = mybir.dt.bfloat16
I32 = mybir.dt.int32
U32 = mybir.dt.uint32
U8 = mybir.dt.uint8
E4M3_X4 = mybir.dt.float8_e4m3fn_x4
E5M2_X4 = mybir.dt.float8_e5m2_x4
ALU = mybir.AluOpType
ACT = mybir.ActivationFunctionType
AXIS = mybir.AxisListType

B = 2
C = 256
N = 8192

P = 128
PACK = 4
PAIRS = PACK // 2
K_PASS = P * PACK
PASSES = N // K_PASS
C_TILES = C // P
ROW_TILES = B * C_TILES
MOVING = 2 * C

ROUND = 2
ROUNDS_PER_BATCH = PASSES // ROUND
ROUNDS = B * ROUNDS_PER_BATCH
X_LOAD_ROUNDS = 2
X_LOAD_N = X_LOAD_ROUNDS * ROUND * K_PASS
X_LOADS = ROUNDS // X_LOAD_ROUNDS

X_AHEAD = 2
MX_BEHIND = 2

G_COLS_VECTOR = 144
RUN = 4

FLOPS = 2 * B * C * C * N
BYTES = 2 * B * C * C + 2 * 2 * B * C * N + 4 * B * C * C


def tile_interfusion_pb_k_kernel(tc, logits1, logits2, x1, x2, grad_out, out):
    nc = tc.nc
    with ExitStack() as ctx:
        ctx.enter_context(tc.manual_schedule())
        resident = ctx.enter_context(tc.tile_pool(name="resident", bufs=1))
        stage = ctx.enter_context(tc.tile_pool(name="stage", bufs=3))
        results = ctx.enter_context(tc.tile_pool(name="results", bufs=2))
        xt_banks = ctx.enter_context(tc.psum_pool(name="xt_banks", bufs=2 * ROUND))
        d_banks = ctx.enter_context(tc.psum_pool(name="d_banks", bufs=B))

        logits = resident.tile([P, ROW_TILES, C], BF16)
        nc.sync.dma_start(out=logits[:], in_=logits1.rearrange("b (ct p) j -> p (b ct) j", p=P))

        x_view = x1.rearrange("b (ct p) h w -> b p ct (h w)", p=P)
        x_raw = {}

        def load_x(load):
            b, part = divmod(load, X_LOADS // B)
            tile = resident.tile([P, C_TILES * X_LOAD_N], BF16, name="x_raw%d" % load)
            nc.sync.dma_start(
                out=tile[:].rearrange("p (ct n) -> p ct n", ct=C_TILES),
                in_=x_view[b, :, :, part * X_LOAD_N : (part + 1) * X_LOAD_N],
            )
            x_raw[load] = tile

        g_view = grad_out.rearrange("b a h w -> b (a h w)").rearrange(
            "b (r j q t c) -> b r j q (t c)", j=ROUND, q=P, t=PACK, c=C
        )
        g_raw = {}

        def load_g(r):
            b, r_in_batch = divmod(r, ROUNDS_PER_BATCH)
            tile = resident.tile([P, ROUND, PACK, C], BF16, name="g_raw%d" % r)
            for j in range(ROUND):
                nc.sync.dma_start(out=tile[:, j].rearrange("p t c -> p (t c)"), in_=g_view[b, r_in_batch, j])
            g_raw[r] = tile

        load_x(0)
        for load in range(X_LOADS):
            if load + 1 < X_LOADS:
                load_x(load + 1)
            for r in range(load * X_LOAD_ROUNDS, (load + 1) * X_LOAD_ROUNDS):
                load_g(r)

        identity = resident.tile([P, P], F32)
        make_identity(nc, identity[:])

        x_codes = {}
        x_scales = {}
        for b in range(B):
            codes = resident.tile([P, (PASSES + 1) * C], U32, name="x_codes%d" % b, align_bytes=64)
            scales = resident.tile([P, (PASSES + 1) * C], U8, name="x_scales%d" % b, align_bytes=64)
            nc.vector.memset(codes[:].bitcast(I32)[:, 0:C], 0)
            nc.vector.memset(scales[:].bitcast(I32)[:, 0 : C // 4], 0)
            x_codes[b] = codes
            x_scales[b] = scales

        row_max = resident.tile([P, ROW_TILES], F32)
        neg_max = resident.tile([P, ROW_TILES], F32)
        row_sum = resident.tile([P, ROW_TILES], F32)
        inv_sum = resident.tile([P, ROW_TILES], F32)
        prob = resident.tile([P, ROW_TILES, C], F32)
        nc.vector.tensor_reduce(out=row_max[:], in_=logits[:], axis=AXIS.X, op=ALU.max)
        nc.vector.tensor_scalar_mul(out=neg_max[:], in0=row_max[:], scalar1=-1.0)
        for m in range(ROW_TILES):
            nc.scalar.activation(
                out=prob[:, m, :],
                in_=logits[:, m, :],
                func=ACT.Exp,
                bias=neg_max[:, m : m + 1],
                scale=1.0,
                accum_out=row_sum[:, m : m + 1],
            )
        nc.vector.reciprocal(out=inv_sum[:], in_=row_sum[:])
        for m in range(ROW_TILES):
            nc.vector.tensor_scalar_mul(out=prob[:, m, :], in0=prob[:, m, :], scalar1=inv_sum[:, m : m + 1])

        xt = {}
        x_grouped = {}
        g_grouped = {}
        g_codes = {}
        g_scales = {}
        d_acc = {}

        def transpose_x(r):
            words = x_raw[r // X_LOAD_ROUNDS][:].bitcast(F32).rearrange("p (q u) -> p q u", u=PAIRS)
            for j in range(ROUND):
                bank = xt_banks.tile([P, PAIRS, C], F32)
                pass_in_load = (r % X_LOAD_ROUNDS) * ROUND + j
                for u in range(PAIRS):
                    for ct in range(C_TILES):
                        first_q = ct * (X_LOAD_N // PACK) + pass_in_load * P
                        nc.tensor.transpose(
                            bank[:, u, ct * P : (ct + 1) * P], words[:, first_q : first_q + P, u], identity[:]
                        )
                xt[(r, j)] = bank

        def copy_x(r):
            grouped = stage.tile([P, ROUND * C * PACK], BF16, name="x_grouped", align_bytes=64)
            grouped_words = grouped[:].bitcast(F32).rearrange("p (j k u) -> p j k u", j=ROUND, u=PAIRS)
            for j in range(ROUND):
                nc.scalar.copy(out=grouped_words[:, j], in_=xt[(r, j)][:].rearrange("p u k -> p k u"))
            x_grouped[r] = grouped

        def regroup_g(r, engine_copy, columns):
            for j in range(ROUND):
                engine_copy(
                    out=g_grouped[r][:, j, columns, :].rearrange("p (c i) t -> p c t i", i=RUN),
                    in_=g_raw[r][:, j, :, columns].rearrange("p t (c i) -> p c t i", i=RUN),
                )

        def regroup_g_scalar(r):
            grouped = stage.tile([P, ROUND, C, PACK], BF16, name="g_grouped", align_bytes=64)
            g_grouped[r] = grouped
            regroup_g(r, nc.scalar.copy, slice(G_COLS_VECTOR, C))

        def regroup_g_vector(r):
            regroup_g(r, nc.vector.tensor_copy, slice(0, G_COLS_VECTOR))

        def quantise_x(r):
            b, r_in_batch = divmod(r, ROUNDS_PER_BATCH)
            slots = slice((1 + r_in_batch * ROUND) * C, (1 + (r_in_batch + 1) * ROUND) * C)
            nc.vector.quantize_mx(
                out=x_codes[b][:, slots].bitcast(E4M3_X4), scales=x_scales[b][:, slots], in_=x_grouped[r][:]
            )

        def quantise_g(r):
            codes = stage.tile([P, ROUND * C], U32, name="g_codes", align_bytes=64)
            scales = stage.tile([P, ROUND * C], U8, name="g_scales", align_bytes=64)
            for j in range(ROUND):
                nc.vector.quantize_mx(
                    out=codes[:, j * C : (j + 1) * C].bitcast(E5M2_X4),
                    scales=scales[:, j * C : (j + 1) * C],
                    in_=g_grouped[r][:, j].rearrange("p c t -> p (c t)"),
                )
            g_codes[r] = codes
            g_scales[r] = scales

        def multiply(r):
            b, r_in_batch = divmod(r, ROUNDS_PER_BATCH)
            if r_in_batch == 0:
                for ct in range(C_TILES):
                    acc = d_banks.tile([P, MOVING], F32, name="d_acc%d" % ct)
                    d_acc[(b, ct)] = acc
            for j in range(ROUND):
                k_pass = r_in_batch * ROUND + j
                window = slice(k_pass * C, k_pass * C + MOVING)
                for ct in range(C_TILES):
                    rows = slice(j * C + ct * P, j * C + (ct + 1) * P)
                    nc.tensor.matmul_mx(
                        out=d_acc[(b, ct)][:],
                        lhsT=g_codes[r][:, rows].bitcast(E5M2_X4),
                        lhsT_scale=g_scales[r][:, rows],
                        rhs=x_codes[b][:, window].bitcast(E4M3_X4),
                        rhs_scale=x_scales[b][:, window],
                        start=(k_pass == 0),
                        stop=(k_pass == PASSES - 1),
                    )

        dot = resident.tile([P, ROW_TILES], F32)

        def finish(b):
            for ct in range(C_TILES):
                m = b * C_TILES + ct
                weighted = results.tile([P, C], F32, name="weighted")
                nc.vector.scalar_tensor_tensor(
                    out=weighted[:],
                    in0=d_acc[(b, ct)][:, C:MOVING],
                    scalar=1.0,
                    in1=prob[:, m, :],
                    op0=ALU.mult,
                    op1=ALU.mult,
                    accum_out=dot[:, m : m + 1],
                )
            for ct in range(C_TILES):
                m = b * C_TILES + ct
                result = results.tile([P, C], F32, name="result")
                nc.vector.scalar_tensor_tensor(
                    out=result[:],
                    in0=d_acc[(b, ct)][:, C:MOVING],
                    scalar=dot[:, m : m + 1],
                    in1=prob[:, m, :],
                    op0=ALU.subtract,
                    op1=ALU.mult,
                )
                nc.sync.dma_start(out=out[b, ct * P : (ct + 1) * P, :], in_=result[:])

        def live(r):
            return 0 <= r < ROUNDS

        for s in range(-X_AHEAD, ROUNDS + MX_BEHIND):
            if live(s - MX_BEHIND):
                multiply(s - MX_BEHIND)
            if live(s + X_AHEAD):
                transpose_x(s + X_AHEAD)
            if live(s + X_AHEAD - 1):
                copy_x(s + X_AHEAD - 1)
            if live(s):
                regroup_g_scalar(s)
                quantise_x(s)
            if live(s - 1):
                quantise_g(s - 1)
            if live(s):
                regroup_g_vector(s)
            if live(s - MX_BEHIND) and (s - MX_BEHIND) % ROUNDS_PER_BATCH == ROUNDS_PER_BATCH - 1:
                finish((s - MX_BEHIND) // ROUNDS_PER_BATCH)
